import numpy as np
import ml_dtypes


def mxq(x, axis, fmt="e4m3"):
    dtype, down = {"e4m3": (ml_dtypes.float8_e4m3fn, 7), "e5m2": (ml_dtypes.float8_e5m2, 14)}[fmt]
    v = np.moveaxis(np.asarray(x, np.float32).astype(ml_dtypes.bfloat16).astype(np.float64), axis, -1)
    blocks = v.reshape(v.shape[:-1] + (-1, 32))
    amax = np.abs(blocks).max(-1, keepdims=True)
    byte = np.maximum(np.where(amax > 0, np.frexp(amax)[1] - 1 + 127, 0) - down, 1)
    scale = np.exp2(byte - 127.0)
    codes = (blocks / scale).astype(np.float32).astype(dtype).astype(np.float64)
    return np.moveaxis((codes * scale).reshape(v.shape), -1, axis)


BF16 = ml_dtypes.bfloat16


def bf(x):
    return np.asarray(x, np.float32).astype(BF16)


def f64(x):
    return np.asarray(x).astype(np.float64)


B, C, H, W = 16, 128, 32, 32
N = H * W
A = np.sqrt(3.0 / np.sqrt(C))


def sigmoid(v):
    return 1.0 / (1.0 + np.exp(-v))


def setup_inputs():
    q = np.random.standard_normal((B, C, H, W)) * A
    s = np.random.standard_normal((B, C, H, W)) * A
    s = s - s.mean(axis=(2, 3), keepdims=True) + np.random.standard_normal((B, C, 1, 1)) * 1.5 / (A * np.sqrt(C) * N)
    return {"query_feature": bf(q), "support_feature": bf(s)}


def reference(query_feature, support_feature):
    q, s = f64(query_feature), f64(support_feature)
    qf = q.reshape(B, N, C)
    sf = s.reshape(B, C, N)
    adj = qf @ sf
    e = np.exp(adj - adj.max(-1, keepdims=True))
    logits = (mxq(e, 2, "e4m3") @ mxq(qf, 1, "e4m3")) / e.sum(-1, keepdims=True)
    gate = sigmoid(adj.sum(-1))
    logits = logits * gate[..., None]
    sup = s.reshape(B, N, C) * gate[..., None]
    return (q + logits.reshape(B, C, H, W), s + sup.reshape(B, C, H, W))

@@ -1,0 +1,271 @@
+from contextlib import ExitStack
+
+import concourse.mybir as mybir
+from concourse.masks import make_identity
+
+F32 = mybir.dt.float32
+BF16 = mybir.dt.bfloat16
+U32 = mybir.dt.uint32
+U8 = mybir.dt.uint8
+FP8X4 = mybir.dt.float8_e4m3fn_x4
+ACTF = mybir.ActivationFunctionType
+ALU = mybir.AluOpType
+AX = mybir.AxisListType
+
+B = 16
+P = 128
+N = 1024
+C = 128
+T = N // P
+NT = B * T
+FLOPS = 2 * 2 * B * N * N * C
+
+PIN = False
+DVE_CP = (3, 7)
+
+
+def tile_fusionfeature_layer_t_kernel(tc, query_feature, support_feature, out_0, out_1):
+    nc = tc.nc
+    q_dram = query_feature.rearrange("b c h w -> b c (h w)")
+    s_dram = support_feature.rearrange("b c h w -> b c (h w)")
+    q2_dram = query_feature.rearrange("b (j ph) (pl xh) w -> b (ph pl) j (xh w)", j=8, pl=8)
+    o0_dram = out_0.rearrange("b c h w -> b c (h w)")
+    o1_dram = out_1.rearrange("b c h w -> b c (h w)")
+
+    with ExitStack() as ctx:
+        const = ctx.enter_context(tc.tile_pool(name="const", bufs=1))
+        inp = ctx.enter_context(tc.tile_pool(name="inp", bufs=4))
+        prep = ctx.enter_context(tc.tile_pool(name="prep", bufs=2))
+        small = ctx.enter_context(tc.tile_pool(name="small", bufs=3))
+        work = ctx.enter_context(tc.tile_pool(name="work", bufs=3))
+        nap = ctx.enter_context(tc.tile_pool(name="nap", bufs=4))
+        outp = ctx.enter_context(tc.tile_pool(name="outp", bufs=2))
+        adjp = ctx.enter_context(tc.psum_pool(name="adjp", bufs=3))
+        auxp = ctx.enter_context(tc.psum_pool(name="auxp", bufs=3))
+        lgp = ctx.enter_context(tc.psum_pool(name="lgp", bufs=2))
+        if PIN:
+            ctx.enter_context(tc.manual_schedule())
+
+        ident = const.tile([P, P], BF16, name="ident")
+        make_identity(nc, ident[:])
+        junk = const.tile([P, N], BF16, name="junk")
+
+        st = {}
+
+        def load(b):
+            q_sb = inp.tile([P, T, C], BF16, name="q_sb", tag="q")
+            s_sb = inp.tile([P, N], BF16, name="s_sb", tag="s")
+            q2 = inp.tile([P, 2, 4, C], BF16, name="q2", tag="q2")
+            nc.sync.dma_start(out=q_sb[:].rearrange("p t c -> p (t c)"), in_=q_dram[b])
+            nc.sync.dma_start(out=s_sb[:], in_=s_dram[b])
+            nc.sync.dma_start(out=q2[:].rearrange("p g j c -> p (g j) c"), in_=q2_dram[b])
+            st[("q", b)] = q_sb
+            st[("s", b)] = s_sb
+            st[("q2", b)] = q2
+
+        def prep_a(b):
+            q_sb = st[("q", b)]
+            qT_ps = auxp.tile([P, T, P], BF16, name="qT_ps", tag="aux")
+            for t in range(T):
+                nc.tensor.transpose(qT_ps[:, t, :], q_sb[:, t, :], ident[:])
+            qT = prep.tile([P, T, P], BF16, name="qT", tag="qT")
+            nc.scalar.copy(out=qT[:], in_=qT_ps[:])
+            st[("qT", b)] = qT
+
+        def prep_b(b):
+            q2 = st[("q2", b)]
+            qg = prep.tile([P, 2, C, 4], BF16, name="qg", tag="qg", align_bytes=64)
+            for g in range(2):
+                nc.gpsimd.tensor_scalar(
+                    out=qg[:, g], in0=q2[:, g].rearrange("p j c -> p c j"),
+                    scalar1=1.0, scalar2=0.0, op0=ALU.mult, op1=ALU.add,
+                )
+            st[("qg", b)] = qg
+            ssum = small.tile([P, 1], F32, name="ssum", tag="ssum")
+            nc.vector.tensor_scalar(
+                out=junk[:], in0=st[("s", b)][:], scalar1=1.0, scalar2=None,
+                op0=ALU.mult, op1=ALU.add, accum_out=ssum[:],
+            )
+            st[("ssum", b)] = ssum
+
+        def prep_c(b):
+            qg = st[("qg", b)]
+            qc = prep.tile([P, 2 * C], U32, name="qc", tag="qc", align_bytes=64)
+            qs = prep.tile([P, 2 * C], U8, name="qs", tag="qs", align_bytes=64)
+            nc.vector.quantize_mx(
+                out=qc[:].bitcast(FP8X4), scales=qs[:], in_=qg[:].rearrange("p g c j -> p (g c j)")
+            )
+            st[("qc", b)] = qc
+            st[("qs", b)] = qs
+            ssum = st[("ssum", b)]
+            ss3 = small.tile([P, 4], BF16, name="ss3", tag="ss3")
+            rr = small.tile([P, 2], F32, name="rr", tag="rr")
+            nc.gpsimd.tensor_copy(out=ss3[:, 0:1], in_=ssum[:])
+            nc.gpsimd.tensor_tensor(out=rr[:, 0:1], in0=ssum[:], in1=ss3[:, 0:1], op=ALU.subtract)
+            nc.gpsimd.tensor_copy(out=ss3[:, 1:2], in_=rr[:, 0:1])
+            nc.gpsimd.tensor_tensor(out=rr[:, 1:2], in0=rr[:, 0:1], in1=ss3[:, 1:2], op=ALU.subtract)
+            nc.gpsimd.tensor_copy(out=ss3[:, 2:3], in_=rr[:, 1:2])
+            st[("ss3", b)] = ss3
+
+        def prep_d(b):
+            qT = st[("qT", b)]
+            ss3 = st[("ss3", b)]
+            v_ps = auxp.tile([P, T, 4], F32, name="v_ps", tag="aux")
+            for t in range(T):
+                nc.tensor.matmul(v_ps[:, t, 0:3], lhsT=qT[:, t, :], rhs=ss3[:, 0:3], start=True, stop=True)
+            v = small.tile([P, T], F32, name="v", tag="v")
+            nc.vector.tensor_reduce(out=v[:], in_=v_ps[:, :, 0:3], axis=AX.X, op=ALU.add)
+            en = small.tile([P, T], F32, name="en", tag="en")
+            nc.scalar.activation(out=en[:], in_=v[:], func=ACTF.Exp, scale=-1.0)
+            d = small.tile([P, T], F32, name="d", tag="d")
+            nc.vector.tensor_scalar_add(out=d[:], in0=en[:], scalar1=1.0)
+            gate = small.tile([P, T], F32, name="gate", tag="gate")
+            nc.vector.reciprocal(out=gate[:], in_=d[:])
+            gate1 = small.tile([P, T], F32, name="gate1", tag="gate1")
+            nc.gpsimd.tensor_scalar(out=gate1[:], in0=gate[:], scalar1=1.0, scalar2=1.0, op0=ALU.mult, op1=ALU.add)
+            st[("d", b)] = d
+            st[("gate1", b)] = gate1
+            rs = small.tile([P, T], F32, name="rs", tag="rs")
+            st[("rs", b)] = rs
+
+        def out1(b):
+            s_sb = st[("s", b)]
+            gate1 = st[("gate1", b)]
+            o1 = outp.tile([P, T, C], F32, name="o1", tag="o1")
+            for t in range(T):
+                nc.gpsimd.tensor_scalar(
+                    out=o1[:, t, :], in0=s_sb[:, t * C:(t + 1) * C],
+                    scalar1=gate1[:, t:t + 1], scalar2=0.0, op0=ALU.mult, op1=ALU.add,
+                )
+            nc.sync.dma_start(out=o1_dram[b], in_=o1[:].rearrange("p t c -> p (t c)"))
+
+        def adj(i):
+            b, t = divmod(i, T)
+            qT = st[("qT", b)]
+            s_sb = st[("s", b)]
+            for h in range(2):
+                a = adjp.tile([P, 512], F32, name="adj_ps", tag="adj")
+                nc.tensor.matmul(a[:], lhsT=qT[:, t, :], rhs=s_sb[:, h * 512:(h + 1) * 512], start=True, stop=True)
+                st[("adj", i, h)] = a
+
+        def max_half(i, h):
+            if h == 0:
+                st[("na", i)] = nap.tile([P, N], F32, name="na", tag="na")
+                st[("nm", i)] = small.tile([P, 2], F32, name="nm", tag="nm", bufs=4)
+            na = st[("na", i)]
+            nm = st[("nm", i)]
+            nc.vector.tensor_scalar(
+                out=na[:, h * 512:(h + 1) * 512], in0=st[("adj", i, h)][:], scalar1=-1.0,
+                scalar2=(None if h == 0 else nm[:, 0:1]), op0=ALU.mult, op1=ALU.min,
+                accum_out=nm[:, h:h + 1],
+            )
+
+        def expo(i):
+            b, t = divmod(i, T)
+            e_sb = work.tile([P, N], BF16, name="e_sb", tag="e")
+            nc.scalar.activation(
+                out=e_sb[:], in_=st[("na", i)][:], func=ACTF.Exp, bias=st[("nm", i)][:, 1:2], scale=-1.0,
+                accum_out=st[("rs", b)][:, t:t + 1],
+            )
+            st[("e", i)] = e_sb
+
+        def trans(i):
+            e_sb = st[("e", i)]
+            xt = auxp.tile([P, T, P], BF16, name="xt", tag="aux")
+            for j in range(8):
+                nc.tensor.transpose(xt[:, j, :], e_sb[:, j * P:(j + 1) * P], ident[:])
+            st[("xt", i)] = xt
+
+        def cpout(i):
+            t = i % T
+            grp = work.tile([P, 2, P, 4], BF16, name="grp", tag="grp", align_bytes=64)
+            src = st[("xt", i)][:].rearrange("p (g j) n -> p g n j", g=2)
+            if t in DVE_CP:
+                nc.vector.tensor_copy(out=grp[:], in_=src)
+            else:
+                nc.scalar.copy(out=grp[:], in_=src)
+            st[("grp", i)] = grp
+
+        def quant(i):
+            ec = work.tile([P, 2 * P], U32, name="ec", tag="ec", align_bytes=64)
+            es = work.tile([P, 2 * P], U8, name="es", tag="es", align_bytes=64)
+            nc.vector.quantize_mx(
+                out=ec[:].bitcast(FP8X4), scales=es[:], in_=st[("grp", i)][:].rearrange("p g n j -> p (g n j)")
+            )
+            st[("ec", i)] = ec
+            st[("es", i)] = es
+
+        def mxmm(i):
+            b, t = divmod(i, T)
+            if t % 4 == 0:
+                st[("lg", b, t // 4)] = lgp.tile([P, 4, C], F32, name="lg", tag="lg")
+            lg = st[("lg", b, t // 4)]
+            ec = st[("ec", i)]
+            es = st[("es", i)]
+            qc = st[("qc", b)]
+            qs = st[("qs", b)]
+            for g in range(2):
+                sl = slice(g * P, (g + 1) * P)
+                nc.tensor.matmul_mx(
+                    out=lg[:, t % 4, :], lhsT=ec[:, sl].bitcast(FP8X4), lhsT_scale=es[:, sl],
+                    rhs=qc[:, sl].bitcast(FP8X4), rhs_scale=qs[:, sl], start=(g == 0), stop=(g == 1),
+                )
+
+        def fin(b, h):
+            sl = slice(4 * h, 4 * h + 4)
+            dr = small.tile([P, 4], F32, name="dr", tag="dr")
+            nc.vector.tensor_tensor(out=dr[:], in0=st[("d", b)][:, sl], in1=st[("rs", b)][:, sl], op=ALU.mult)
+            gg = small.tile([P, 4], F32, name="gg", tag="gg")
+            nc.vector.reciprocal(out=gg[:], in_=dr[:])
+            lg = st[("lg", b, h)]
+            q_sb = st[("q", b)]
+            o0 = outp.tile([P, 4, C], F32, name="o0", tag="o0", bufs=3)
+            for k in range(4):
+                nc.vector.scalar_tensor_tensor(
+                    out=o0[:, k, :], in0=lg[:, k, :], scalar=gg[:, k:k + 1], in1=q_sb[:, 4 * h + k, :],
+                    op0=ALU.mult, op1=ALU.add,
+                )
+            nc.sync.dma_start(out=o0_dram[b][:, h * 512:(h + 1) * 512], in_=o0[:].rearrange("p k c -> p (k c)"))
+
+        load(0)
+        load(1)
+        prep_a(0)
+        prep_b(0)
+        prep_c(0)
+        prep_d(0)
+        for s in range(-2, NT + 4):
+            if 0 <= s - 1 < NT:
+                trans(s - 1)
+            if 0 <= s + 2 < NT:
+                adj(s + 2)
+            if 0 <= s + 1 < NT:
+                max_half(s + 1, 0)
+            if 0 <= s - 2 < NT:
+                quant(s - 2)
+            if 0 <= s + 1 < NT:
+                max_half(s + 1, 1)
+            if 0 <= s < NT:
+                expo(s)
+            if 0 <= s - 1 < NT:
+                cpout(s - 1)
+            if 0 <= s - 2 < NT:
+                mxmm(s - 2)
+            if 0 <= s - 3 < NT and (s - 3) % 4 == 3:
+                fin((s - 3) // T, ((s - 3) % T) // 4)
+            if s >= 0:
+                b, u = divmod(s, T)
+                if u == 0 and b + 2 < B:
+                    load(b + 2)
+                if u == 0 and b == 0:
+                    out1(0)
+                if b + 1 < B:
+                    if u == 1:
+                        prep_a(b + 1)
+                    if u == 2:
+                        prep_b(b + 1)
+                    if u == 3:
+                        prep_c(b + 1)
+                    if u == 4:
+                        prep_d(b + 1)
+                    if u == 5:
+                        out1(b + 1)

@@ -20,8 +20,8 @@ T = N // P
 NT = B * T
 FLOPS = 2 * 2 * B * N * N * C
 
-PIN = False
-DVE_CP = (3, 7)
+PIN = True
+DVE_CP = (1,)
 
 
 def tile_fusionfeature_layer_t_kernel(tc, query_feature, support_feature, out_0, out_1):
@@ -72,7 +72,7 @@ def tile_fusionfeature_layer_t_kernel(tc, query_feature, support_feature, out_0,
             nc.scalar.copy(out=qT[:], in_=qT_ps[:])
             st[("qT", b)] = qT
 
-        def prep_b(b):
+        def prep_regroup(b):
             q2 = st[("q2", b)]
             qg = prep.tile([P, 2, C, 4], BF16, name="qg", tag="qg", align_bytes=64)
             for g in range(2):
@@ -81,6 +81,8 @@ def tile_fusionfeature_layer_t_kernel(tc, query_feature, support_feature, out_0,
                     scalar1=1.0, scalar2=0.0, op0=ALU.mult, op1=ALU.add,
                 )
             st[("qg", b)] = qg
+
+        def prep_ssum(b):
             ssum = small.tile([P, 1], F32, name="ssum", tag="ssum")
             nc.vector.tensor_scalar(
                 out=junk[:], in0=st[("s", b)][:], scalar1=1.0, scalar2=None,
@@ -88,7 +90,7 @@ def tile_fusionfeature_layer_t_kernel(tc, query_feature, support_feature, out_0,
             )
             st[("ssum", b)] = ssum
 
-        def prep_c(b):
+        def prep_quant(b):
             qg = st[("qg", b)]
             qc = prep.tile([P, 2 * C], U32, name="qc", tag="qc", align_bytes=64)
             qs = prep.tile([P, 2 * C], U8, name="qs", tag="qs", align_bytes=64)
@@ -97,6 +99,8 @@ def tile_fusionfeature_layer_t_kernel(tc, query_feature, support_feature, out_0,
             )
             st[("qc", b)] = qc
             st[("qs", b)] = qs
+
+        def prep_split(b):
             ssum = st[("ssum", b)]
             ss3 = small.tile([P, 4], BF16, name="ss3", tag="ss3")
             rr = small.tile([P, 2], F32, name="rr", tag="rr")
@@ -107,37 +111,48 @@ def tile_fusionfeature_layer_t_kernel(tc, query_feature, support_feature, out_0,
             nc.gpsimd.tensor_copy(out=ss3[:, 2:3], in_=rr[:, 1:2])
             st[("ss3", b)] = ss3
 
-        def prep_d(b):
+        def prep_d1(b):
             qT = st[("qT", b)]
             ss3 = st[("ss3", b)]
             v_ps = auxp.tile([P, T, 4], F32, name="v_ps", tag="aux")
             for t in range(T):
                 nc.tensor.matmul(v_ps[:, t, 0:3], lhsT=qT[:, t, :], rhs=ss3[:, 0:3], start=True, stop=True)
+            st[("v_ps", b)] = v_ps
+
+        def prep_d2_dve(b):
             v = small.tile([P, T], F32, name="v", tag="v")
-            nc.vector.tensor_reduce(out=v[:], in_=v_ps[:, :, 0:3], axis=AX.X, op=ALU.add)
+            nc.vector.tensor_reduce(out=v[:], in_=st[("v_ps", b)][:, :, 0:3], axis=AX.X, op=ALU.add)
+            st[("v", b)] = v
+
+        def prep_d2_act(b):
             en = small.tile([P, T], F32, name="en", tag="en")
-            nc.scalar.activation(out=en[:], in_=v[:], func=ACTF.Exp, scale=-1.0)
+            nc.scalar.activation(out=en[:], in_=st[("v", b)][:], func=ACTF.Exp, scale=-1.0)
             d = small.tile([P, T], F32, name="d", tag="d")
-            nc.vector.tensor_scalar_add(out=d[:], in0=en[:], scalar1=1.0)
-            gate = small.tile([P, T], F32, name="gate", tag="gate")
-            nc.vector.reciprocal(out=gate[:], in_=d[:])
-            gate1 = small.tile([P, T], F32, name="gate1", tag="gate1")
-            nc.gpsimd.tensor_scalar(out=gate1[:], in0=gate[:], scalar1=1.0, scalar2=1.0, op0=ALU.mult, op1=ALU.add)
+            nc.gpsimd.tensor_scalar(out=d[:], in0=en[:], scalar1=1.0, scalar2=1.0, op0=ALU.mult, op1=ALU.add)
             st[("d", b)] = d
-            st[("gate1", b)] = gate1
             rs = small.tile([P, T], F32, name="rs", tag="rs")
             st[("rs", b)] = rs
 
-        def out1(b):
+        def prep_d3(b):
+            gate = small.tile([P, T], F32, name="gate", tag="gate")
+            nc.vector.reciprocal(out=gate[:], in_=st[("d", b)][:])
+            gate1 = small.tile([P, T], F32, name="gate1", tag="gate1")
+            nc.gpsimd.tensor_scalar(out=gate1[:], in0=gate[:], scalar1=1.0, scalar2=1.0, op0=ALU.mult, op1=ALU.add)
+            st[("gate1", b)] = gate1
+
+        def out1(b, h):
             s_sb = st[("s", b)]
             gate1 = st[("gate1", b)]
-            o1 = outp.tile([P, T, C], F32, name="o1", tag="o1")
-            for t in range(T):
+            if h == 0:
+                st[("o1", b)] = outp.tile([P, T, C], F32, name="o1", tag="o1")
+            o1 = st[("o1", b)]
+            for t in range(4 * h, 4 * h + 4):
                 nc.gpsimd.tensor_scalar(
                     out=o1[:, t, :], in0=s_sb[:, t * C:(t + 1) * C],
                     scalar1=gate1[:, t:t + 1], scalar2=0.0, op0=ALU.mult, op1=ALU.add,
                 )
-            nc.sync.dma_start(out=o1_dram[b], in_=o1[:].rearrange("p t c -> p (t c)"))
+            if h == 1:
+                nc.sync.dma_start(out=o1_dram[b], in_=o1[:].rearrange("p t c -> p (t c)"))
 
         def adj(i):
             b, t = divmod(i, T)
@@ -211,12 +226,19 @@ def tile_fusionfeature_layer_t_kernel(tc, query_feature, support_feature, out_0,
                     rhs=qc[:, sl].bitcast(FP8X4), rhs_scale=qs[:, sl], start=(g == 0), stop=(g == 1),
                 )
 
-        def fin(b, h):
+        def fin_dr(b, h):
             sl = slice(4 * h, 4 * h + 4)
             dr = small.tile([P, 4], F32, name="dr", tag="dr")
-            nc.vector.tensor_tensor(out=dr[:], in0=st[("d", b)][:, sl], in1=st[("rs", b)][:, sl], op=ALU.mult)
+            nc.gpsimd.tensor_tensor(out=dr[:], in0=st[("d", b)][:, sl], in1=st[("rs", b)][:, sl], op=ALU.mult)
+            st[("dr", b, h)] = dr
+
+        def fin_gg(b, h):
             gg = small.tile([P, 4], F32, name="gg", tag="gg")
-            nc.vector.reciprocal(out=gg[:], in_=dr[:])
+            nc.vector.reciprocal(out=gg[:], in_=st[("dr", b, h)][:])
+            st[("gg", b, h)] = gg
+
+        def fin(b, h):
+            gg = st[("gg", b, h)]
             lg = st[("lg", b, h)]
             q_sb = st[("q", b)]
             o0 = outp.tile([P, 4, C], F32, name="o0", tag="o0", bufs=3)
@@ -230,16 +252,31 @@ def tile_fusionfeature_layer_t_kernel(tc, query_feature, support_feature, out_0,
         load(0)
         load(1)
         prep_a(0)
-        prep_b(0)
-        prep_c(0)
-        prep_d(0)
-        for s in range(-2, NT + 4):
+        prep_ssum(0)
+        prep_split(0)
+        prep_regroup(0)
+        prep_d1(0)
+        prep_d2_dve(0)
+        prep_d2_act(0)
+        prep_d3(0)
+        prep_quant(0)
+        for s in range(-2, NT + 5):
+            b, u = divmod(s, T)
+            nb = b + 1
+            pre = 0 <= s and nb < B
+            done = s - 3
             if 0 <= s - 1 < NT:
                 trans(s - 1)
             if 0 <= s + 2 < NT:
                 adj(s + 2)
             if 0 <= s + 1 < NT:
                 max_half(s + 1, 0)
+            if pre and u == 3:
+                prep_d2_dve(nb)
+            if pre and u == 4:
+                prep_d3(nb)
+            if 0 <= done - 1 < NT and (done - 1) % 4 == 3:
+                fin_gg((done - 1) // T, ((done - 1) % T) // 4)
             if 0 <= s - 2 < NT:
                 quant(s - 2)
             if 0 <= s + 1 < NT:
@@ -250,22 +287,31 @@ def tile_fusionfeature_layer_t_kernel(tc, query_feature, support_feature, out_0,
                 cpout(s - 1)
             if 0 <= s - 2 < NT:
                 mxmm(s - 2)
-            if 0 <= s - 3 < NT and (s - 3) % 4 == 3:
-                fin((s - 3) // T, ((s - 3) % T) // 4)
-            if s >= 0:
-                b, u = divmod(s, T)
-                if u == 0 and b + 2 < B:
-                    load(b + 2)
-                if u == 0 and b == 0:
-                    out1(0)
-                if b + 1 < B:
-                    if u == 1:
-                        prep_a(b + 1)
-                    if u == 2:
-                        prep_b(b + 1)
-                    if u == 3:
-                        prep_c(b + 1)
-                    if u == 4:
-                        prep_d(b + 1)
-                    if u == 5:
-                        out1(b + 1)
+            if 0 <= done < NT and done % 4 == 3:
+                fin_dr(done // T, (done % T) // 4)
+            if 0 <= done - 1 < NT and (done - 1) % 4 == 3:
+                fin((done - 1) // T, ((done - 1) % T) // 4)
+            if 0 <= s and u == 0 and b + 2 < B:
+                load(b + 2)
+            if s == 0:
+                out1(0, 0)
+            if s == 1:
+                out1(0, 1)
+            if pre:
+                if u == 0:
+                    prep_a(nb)
+                    prep_ssum(nb)
+                if u == 1:
+                    prep_split(nb)
+                if u == 2:
+                    prep_d1(nb)
+                if u == 3:
+                    prep_d2_act(nb)
+                if u == 4:
+                    prep_regroup(nb)
+                if u == 5:
+                    prep_quant(nb)
+                if u == 6:
+                    out1(nb, 0)
+                if u == 7:
+                    out1(nb, 1)

@@ -21,7 +21,8 @@ NT = B * T
 FLOPS = 2 * 2 * B * N * N * C
 
 PIN = True
-DVE_CP = (1,)
+LEAD = 2
+DVE_CP = (1, 5)
 
 
 def tile_fusionfeature_layer_t_kernel(tc, query_feature, support_feature, out_0, out_1):
@@ -38,7 +39,7 @@ def tile_fusionfeature_layer_t_kernel(tc, query_feature, support_feature, out_0,
         prep = ctx.enter_context(tc.tile_pool(name="prep", bufs=2))
         small = ctx.enter_context(tc.tile_pool(name="small", bufs=3))
         work = ctx.enter_context(tc.tile_pool(name="work", bufs=3))
-        nap = ctx.enter_context(tc.tile_pool(name="nap", bufs=4))
+        nap = ctx.enter_context(tc.tile_pool(name="nap", bufs=LEAD + 3))
         outp = ctx.enter_context(tc.tile_pool(name="outp", bufs=2))
         adjp = ctx.enter_context(tc.psum_pool(name="adjp", bufs=3))
         auxp = ctx.enter_context(tc.psum_pool(name="auxp", bufs=3))
@@ -130,8 +131,6 @@ def tile_fusionfeature_layer_t_kernel(tc, query_feature, support_feature, out_0,
             d = small.tile([P, T], F32, name="d", tag="d")
             nc.gpsimd.tensor_scalar(out=d[:], in0=en[:], scalar1=1.0, scalar2=1.0, op0=ALU.mult, op1=ALU.add)
             st[("d", b)] = d
-            rs = small.tile([P, T], F32, name="rs", tag="rs")
-            st[("rs", b)] = rs
 
         def prep_d3(b):
             gate = small.tile([P, T], F32, name="gate", tag="gate")
@@ -166,7 +165,7 @@ def tile_fusionfeature_layer_t_kernel(tc, query_feature, support_feature, out_0,
         def max_half(i, h):
             if h == 0:
                 st[("na", i)] = nap.tile([P, N], F32, name="na", tag="na")
-                st[("nm", i)] = small.tile([P, 2], F32, name="nm", tag="nm", bufs=4)
+                st[("nm", i)] = small.tile([P, 2], F32, name="nm", tag="nm", bufs=LEAD + 3)
             na = st[("na", i)]
             nm = st[("nm", i)]
             nc.vector.tensor_scalar(
@@ -177,6 +176,8 @@ def tile_fusionfeature_layer_t_kernel(tc, query_feature, support_feature, out_0,
 
         def expo(i):
             b, t = divmod(i, T)
+            if t == 0:
+                st[("rs", b)] = small.tile([P, T], F32, name="rs", tag="rs")
             e_sb = work.tile([P, N], BF16, name="e_sb", tag="e")
             nc.scalar.activation(
                 out=e_sb[:], in_=st[("na", i)][:], func=ACTF.Exp, bias=st[("nm", i)][:, 1:2], scale=-1.0,
@@ -249,69 +250,71 @@ def tile_fusionfeature_layer_t_kernel(tc, query_feature, support_feature, out_0,
                 )
             nc.sync.dma_start(out=o0_dram[b][:, h * 512:(h + 1) * 512], in_=o0[:].rearrange("p k c -> p (k c)"))
 
+        def prep_step(b, u):
+            if u == 0 and b > 0:
+                prep_a(b)
+            if u == 0:
+                prep_ssum(b)
+            if u == 1:
+                prep_split(b)
+            if u == 2:
+                prep_regroup(b)
+                prep_d1(b)
+            if u == 3:
+                prep_d2_act(b)
+            if u == 4:
+                prep_quant(b)
+            if u == 6:
+                out1(b, 0)
+            if u == 7:
+                out1(b, 1)
+
+        def prep_step_dve(b, u):
+            if u == 3:
+                prep_d2_dve(b)
+            if u == 5:
+                prep_d3(b)
+
+        first = -LEAD - 1
         load(0)
         load(1)
         prep_a(0)
-        prep_ssum(0)
-        prep_split(0)
-        prep_regroup(0)
-        prep_d1(0)
-        prep_d2_dve(0)
-        prep_d2_act(0)
-        prep_d3(0)
-        prep_quant(0)
-        for s in range(-2, NT + 5):
-            b, u = divmod(s, T)
-            nb = b + 1
-            pre = 0 <= s and nb < B
-            done = s - 3
+        for s in range(first, NT + 7):
+            preps = []
+            if 0 <= s - first - 1 < T:
+                preps.append((0, s - first - 1))
+            if s >= 2:
+                pb, pu = divmod(s - 2, T)
+                if pb + 1 < B:
+                    preps.append((pb + 1, pu))
             if 0 <= s - 1 < NT:
                 trans(s - 1)
-            if 0 <= s + 2 < NT:
-                adj(s + 2)
-            if 0 <= s + 1 < NT:
-                max_half(s + 1, 0)
-            if pre and u == 3:
-                prep_d2_dve(nb)
-            if pre and u == 4:
-                prep_d3(nb)
-            if 0 <= done - 1 < NT and (done - 1) % 4 == 3:
-                fin_gg((done - 1) // T, ((done - 1) % T) // 4)
-            if 0 <= s - 2 < NT:
-                quant(s - 2)
-            if 0 <= s + 1 < NT:
-                max_half(s + 1, 1)
+            if 0 <= s + LEAD + 1 < NT:
+                adj(s + LEAD + 1)
+            if 0 <= s - 4 < NT:
+                mxmm(s - 4)
+            if 0 <= s + LEAD < NT:
+                max_half(s + LEAD, 0)
+            for pb, pu in preps:
+                prep_step_dve(pb, pu)
+            gl = s - 3
+            if 0 <= gl < NT and gl % 4 == 3:
+                fin_gg(gl // T, (gl % T) // 4)
+            if 0 <= s - 3 < NT:
+                quant(s - 3)
+            if 0 <= s + LEAD < NT:
+                max_half(s + LEAD, 1)
             if 0 <= s < NT:
                 expo(s)
-            if 0 <= s - 1 < NT:
-                cpout(s - 1)
             if 0 <= s - 2 < NT:
-                mxmm(s - 2)
-            if 0 <= done < NT and done % 4 == 3:
-                fin_dr(done // T, (done % T) // 4)
-            if 0 <= done - 1 < NT and (done - 1) % 4 == 3:
-                fin((done - 1) // T, ((done - 1) % T) // 4)
-            if 0 <= s and u == 0 and b + 2 < B:
-                load(b + 2)
-            if s == 0:
-                out1(0, 0)
-            if s == 1:
-                out1(0, 1)
-            if pre:
-                if u == 0:
-                    prep_a(nb)
-                    prep_ssum(nb)
-                if u == 1:
-                    prep_split(nb)
-                if u == 2:
-                    prep_d1(nb)
-                if u == 3:
-                    prep_d2_act(nb)
-                if u == 4:
-                    prep_regroup(nb)
-                if u == 5:
-                    prep_quant(nb)
-                if u == 6:
-                    out1(nb, 0)
-                if u == 7:
-                    out1(nb, 1)
+                cpout(s - 2)
+            dl = s - 1
+            if 0 <= dl < NT and dl % 4 == 3:
+                fin_dr(dl // T, (dl % T) // 4)
+            fl = s - 5
+            if 0 <= fl < NT and fl % 4 == 3:
+                fin(fl // T, (fl % T) // 4)
+            if 0 <= s and s % T == 0 and s // T + 2 < B:
+                load(s // T + 2)
+            for pb, pu in preps:
+                prep_step(pb, pu)

@@ -22,7 +22,9 @@ FLOPS = 2 * 2 * B * N * N * C
 
 PIN = True
 LEAD = 2
-DVE_CP = (1, 5)
+DVE_CP = ()
+GP_RG = (0, 3, 4, 5)
+QL = 4
 
 
 def tile_fusionfeature_layer_t_kernel(tc, query_feature, support_feature, out_0, out_1):
@@ -76,11 +78,10 @@ def tile_fusionfeature_layer_t_kernel(tc, query_feature, support_feature, out_0,
         def prep_regroup(b):
             q2 = st[("q2", b)]
             qg = prep.tile([P, 2, C, 4], BF16, name="qg", tag="qg", align_bytes=64)
-            for g in range(2):
-                nc.gpsimd.tensor_scalar(
-                    out=qg[:, g], in0=q2[:, g].rearrange("p j c -> p c j"),
-                    scalar1=1.0, scalar2=0.0, op0=ALU.mult, op1=ALU.add,
-                )
+            nc.gpsimd.tensor_scalar(
+                out=qg[:], in0=q2[:].rearrange("p g j c -> p g c j"),
+                scalar1=1.0, scalar2=0.0, op0=ALU.mult, op1=ALU.add,
+            )
             st[("qg", b)] = qg
 
         def prep_ssum(b):
@@ -194,9 +195,16 @@ def tile_fusionfeature_layer_t_kernel(tc, query_feature, support_feature, out_0,
 
         def cpout(i):
             t = i % T
-            grp = work.tile([P, 2, P, 4], BF16, name="grp", tag="grp", align_bytes=64)
+            grp = work.tile([P, 2, P, 4], BF16, name="grp", tag="grp", align_bytes=64, bufs=QL + 1)
             src = st[("xt", i)][:].rearrange("p (g j) n -> p g n j", g=2)
-            if t in DVE_CP:
+            if t in GP_RG:
+                xs = work.tile([P, T, P], BF16, name="xs", tag="xs")
+                nc.scalar.copy(out=xs[:], in_=st[("xt", i)][:])
+                nc.gpsimd.tensor_scalar(
+                    out=grp[:], in0=xs[:].rearrange("p (g j) n -> p g n j", g=2),
+                    scalar1=1.0, scalar2=0.0, op0=ALU.mult, op1=ALU.add,
+                )
+            elif t in DVE_CP:
                 nc.vector.tensor_copy(out=grp[:], in_=src)
             else:
                 nc.scalar.copy(out=grp[:], in_=src)
@@ -279,7 +287,7 @@ def tile_fusionfeature_layer_t_kernel(tc, query_feature, support_feature, out_0,
         load(0)
         load(1)
         prep_a(0)
-        for s in range(first, NT + 7):
+        for s in range(first, NT + QL + 4):
             preps = []
             if 0 <= s - first - 1 < T:
                 preps.append((0, s - first - 1))
@@ -291,17 +299,17 @@ def tile_fusionfeature_layer_t_kernel(tc, query_feature, support_feature, out_0,
                 trans(s - 1)
             if 0 <= s + LEAD + 1 < NT:
                 adj(s + LEAD + 1)
-            if 0 <= s - 4 < NT:
-                mxmm(s - 4)
+            if 0 <= s - QL - 1 < NT:
+                mxmm(s - QL - 1)
             if 0 <= s + LEAD < NT:
                 max_half(s + LEAD, 0)
             for pb, pu in preps:
                 prep_step_dve(pb, pu)
-            gl = s - 3
+            gl = s - QL
             if 0 <= gl < NT and gl % 4 == 3:
                 fin_gg(gl // T, (gl % T) // 4)
-            if 0 <= s - 3 < NT:
-                quant(s - 3)
+            if 0 <= s - QL < NT:
+                quant(s - QL)
             if 0 <= s + LEAD < NT:
                 max_half(s + LEAD, 1)
             if 0 <= s < NT:
@@ -311,7 +319,7 @@ def tile_fusionfeature_layer_t_kernel(tc, query_feature, support_feature, out_0,
             dl = s - 1
             if 0 <= dl < NT and dl % 4 == 3:
                 fin_dr(dl // T, (dl % T) // 4)
-            fl = s - 5
+            fl = s - QL - 2
             if 0 <= fl < NT and fl % 4 == 3:
                 fin(fl // T, (fl % T) // 4)
             if 0 <= s and s % T == 0 and s // T + 2 < B:

@@ -22,9 +22,8 @@ FLOPS = 2 * 2 * B * N * N * C
 
 PIN = True
 LEAD = 2
-DVE_CP = ()
-GP_RG = (0, 3, 4, 5)
-QL = 4
+DVE_CP = (1,)
+SPLIT_CP = (5,)
 
 
 def tile_fusionfeature_layer_t_kernel(tc, query_feature, support_feature, out_0, out_1):
@@ -78,10 +77,11 @@ def tile_fusionfeature_layer_t_kernel(tc, query_feature, support_feature, out_0,
         def prep_regroup(b):
             q2 = st[("q2", b)]
             qg = prep.tile([P, 2, C, 4], BF16, name="qg", tag="qg", align_bytes=64)
-            nc.gpsimd.tensor_scalar(
-                out=qg[:], in0=q2[:].rearrange("p g j c -> p g c j"),
-                scalar1=1.0, scalar2=0.0, op0=ALU.mult, op1=ALU.add,
-            )
+            for g in range(2):
+                nc.gpsimd.tensor_scalar(
+                    out=qg[:, g], in0=q2[:, g].rearrange("p j c -> p c j"),
+                    scalar1=1.0, scalar2=0.0, op0=ALU.mult, op1=ALU.add,
+                )
             st[("qg", b)] = qg
 
         def prep_ssum(b):
@@ -195,15 +195,11 @@ def tile_fusionfeature_layer_t_kernel(tc, query_feature, support_feature, out_0,
 
         def cpout(i):
             t = i % T
-            grp = work.tile([P, 2, P, 4], BF16, name="grp", tag="grp", align_bytes=64, bufs=QL + 1)
+            grp = work.tile([P, 2, P, 4], BF16, name="grp", tag="grp", align_bytes=64)
             src = st[("xt", i)][:].rearrange("p (g j) n -> p g n j", g=2)
-            if t in GP_RG:
-                xs = work.tile([P, T, P], BF16, name="xs", tag="xs")
-                nc.scalar.copy(out=xs[:], in_=st[("xt", i)][:])
-                nc.gpsimd.tensor_scalar(
-                    out=grp[:], in0=xs[:].rearrange("p (g j) n -> p g n j", g=2),
-                    scalar1=1.0, scalar2=0.0, op0=ALU.mult, op1=ALU.add,
-                )
+            if t in SPLIT_CP:
+                nc.scalar.copy(out=grp[:, 0], in_=src[:, 0])
+                nc.vector.tensor_copy(out=grp[:, 1], in_=src[:, 1])
             elif t in DVE_CP:
                 nc.vector.tensor_copy(out=grp[:], in_=src)
             else:
@@ -287,7 +283,7 @@ def tile_fusionfeature_layer_t_kernel(tc, query_feature, support_feature, out_0,
         load(0)
         load(1)
         prep_a(0)
-        for s in range(first, NT + QL + 4):
+        for s in range(first, NT + 7):
             preps = []
             if 0 <= s - first - 1 < T:
                 preps.append((0, s - first - 1))
@@ -299,17 +295,17 @@ def tile_fusionfeature_layer_t_kernel(tc, query_feature, support_feature, out_0,
                 trans(s - 1)
             if 0 <= s + LEAD + 1 < NT:
                 adj(s + LEAD + 1)
-            if 0 <= s - QL - 1 < NT:
-                mxmm(s - QL - 1)
+            if 0 <= s - 4 < NT:
+                mxmm(s - 4)
             if 0 <= s + LEAD < NT:
                 max_half(s + LEAD, 0)
             for pb, pu in preps:
                 prep_step_dve(pb, pu)
-            gl = s - QL
+            gl = s - 3
             if 0 <= gl < NT and gl % 4 == 3:
                 fin_gg(gl // T, (gl % T) // 4)
-            if 0 <= s - QL < NT:
-                quant(s - QL)
+            if 0 <= s - 3 < NT:
+                quant(s - 3)
             if 0 <= s + LEAD < NT:
                 max_half(s + LEAD, 1)
             if 0 <= s < NT:
@@ -319,7 +315,7 @@ def tile_fusionfeature_layer_t_kernel(tc, query_feature, support_feature, out_0,
             dl = s - 1
             if 0 <= dl < NT and dl % 4 == 3:
                 fin_dr(dl // T, (dl % T) // 4)
-            fl = s - QL - 2
+            fl = s - 5
             if 0 <= fl < NT and fl % 4 == 3:
                 fin(fl // T, (fl % T) // 4)
             if 0 <= s and s % T == 0 and s // T + 2 < B:

@@ -51,6 +51,9 @@ def tile_fusionfeature_layer_t_kernel(tc, query_feature, support_feature, out_0,
         ident = const.tile([P, P], BF16, name="ident")
         make_identity(nc, ident[:])
         junk = const.tile([P, N], BF16, name="junk")
+        warm = const.tile([P, 2], F32, name="warm")
+        nc.vector.memset(warm[:, 0:1], 0.0)
+        nc.scalar.activation(out=warm[:, 1:2], in_=warm[:, 0:1], func=ACTF.Exp)
 
         st = {}
 
@@ -65,14 +68,15 @@ def tile_fusionfeature_layer_t_kernel(tc, query_feature, support_feature, out_0,
             st[("s", b)] = s_sb
             st[("q2", b)] = q2
 
-        def prep_a(b):
+        def prep_a(b, lo, hi):
             q_sb = st[("q", b)]
+            if lo == 0:
+                st[("qT", b)] = prep.tile([P, T, P], BF16, name="qT", tag="qT")
+            qT = st[("qT", b)]
             qT_ps = auxp.tile([P, T, P], BF16, name="qT_ps", tag="aux")
-            for t in range(T):
+            for t in range(lo, hi):
                 nc.tensor.transpose(qT_ps[:, t, :], q_sb[:, t, :], ident[:])
-            qT = prep.tile([P, T, P], BF16, name="qT", tag="qT")
-            nc.scalar.copy(out=qT[:], in_=qT_ps[:])
-            st[("qT", b)] = qT
+            nc.scalar.copy(out=qT[:, lo:hi, :], in_=qT_ps[:, lo:hi, :])
 
         def prep_regroup(b):
             q2 = st[("q2", b)]
@@ -197,10 +201,10 @@ def tile_fusionfeature_layer_t_kernel(tc, query_feature, support_feature, out_0,
             t = i % T
             grp = work.tile([P, 2, P, 4], BF16, name="grp", tag="grp", align_bytes=64)
             src = st[("xt", i)][:].rearrange("p (g j) n -> p g n j", g=2)
-            if t in SPLIT_CP:
+            if i == NT - 1 or (t in SPLIT_CP and i < NT - 3):
                 nc.scalar.copy(out=grp[:, 0], in_=src[:, 0])
                 nc.vector.tensor_copy(out=grp[:, 1], in_=src[:, 1])
-            elif t in DVE_CP:
+            elif t in DVE_CP or i >= NT - 3:
                 nc.vector.tensor_copy(out=grp[:], in_=src)
             else:
                 nc.scalar.copy(out=grp[:], in_=src)
@@ -256,7 +260,7 @@ def tile_fusionfeature_layer_t_kernel(tc, query_feature, support_feature, out_0,
 
         def prep_step(b, u):
             if u == 0 and b > 0:
-                prep_a(b)
+                prep_a(b, 0, T)
             if u == 0:
                 prep_ssum(b)
             if u == 1:
@@ -282,7 +286,7 @@ def tile_fusionfeature_layer_t_kernel(tc, query_feature, support_feature, out_0,
         first = -LEAD - 1
         load(0)
         load(1)
-        prep_a(0)
+        prep_a(0, 0, 1)
         for s in range(first, NT + 7):
             preps = []
             if 0 <= s - first - 1 < T:
@@ -295,6 +299,8 @@ def tile_fusionfeature_layer_t_kernel(tc, query_feature, support_feature, out_0,
                 trans(s - 1)
             if 0 <= s + LEAD + 1 < NT:
                 adj(s + LEAD + 1)
+            if s == first:
+                prep_a(0, 1, T)
             if 0 <= s - 4 < NT:
                 mxmm(s - 4)
             if 0 <= s + LEAD < NT:

@@ -22,15 +22,14 @@ FLOPS = 2 * 2 * B * N * N * C
 
 PIN = True
 LEAD = 2
-DVE_CP = (1,)
-SPLIT_CP = (5,)
+DVE_CP = ()
 
 
 def tile_fusionfeature_layer_t_kernel(tc, query_feature, support_feature, out_0, out_1):
     nc = tc.nc
     q_dram = query_feature.rearrange("b c h w -> b c (h w)")
     s_dram = support_feature.rearrange("b c h w -> b c (h w)")
-    q2_dram = query_feature.rearrange("b (j ph) (pl xh) w -> b (ph pl) j (xh w)", j=8, pl=8)
+    q2_dram = query_feature.rearrange("b (g ch) (cl tx) w -> b (ch cl) g (tx w)", g=2, cl=2)
     o0_dram = out_0.rearrange("b c h w -> b c (h w)")
     o1_dram = out_1.rearrange("b c h w -> b c (h w)")
 
@@ -50,7 +49,9 @@ def tile_fusionfeature_layer_t_kernel(tc, query_feature, support_feature, out_0,
 
         ident = const.tile([P, P], BF16, name="ident")
         make_identity(nc, ident[:])
-        junk = const.tile([P, N], BF16, name="junk")
+        ident32 = const.tile([P, P], F32, name="ident32")
+        make_identity(nc, ident32[:])
+        junk = const.tile([P, 512], F32, name="junk")
         warm = const.tile([P, 2], F32, name="warm")
         nc.vector.memset(warm[:, 0:1], 0.0)
         nc.scalar.activation(out=warm[:, 1:2], in_=warm[:, 0:1], func=ACTF.Exp)
@@ -63,7 +64,7 @@ def tile_fusionfeature_layer_t_kernel(tc, query_feature, support_feature, out_0,
             q2 = inp.tile([P, 2, 4, C], BF16, name="q2", tag="q2")
             nc.sync.dma_start(out=q_sb[:].rearrange("p t c -> p (t c)"), in_=q_dram[b])
             nc.sync.dma_start(out=s_sb[:], in_=s_dram[b])
-            nc.sync.dma_start(out=q2[:].rearrange("p g j c -> p (g j) c"), in_=q2_dram[b])
+            nc.sync.dma_start(out=q2[:].rearrange("p g j c -> p g (j c)"), in_=q2_dram[b])
             st[("q", b)] = q_sb
             st[("s", b)] = s_sb
             st[("q2", b)] = q2
@@ -90,8 +91,8 @@ def tile_fusionfeature_layer_t_kernel(tc, query_feature, support_feature, out_0,
 
         def prep_ssum(b):
             ssum = small.tile([P, 1], F32, name="ssum", tag="ssum")
-            nc.vector.tensor_scalar(
-                out=junk[:], in0=st[("s", b)][:], scalar1=1.0, scalar2=None,
+            nc.vector.scalar_tensor_tensor(
+                out=junk[:], in0=st[("s", b)][:, 0:512], scalar=1.0, in1=st[("s", b)][:, 512:1024],
                 op0=ALU.mult, op1=ALU.add, accum_out=ssum[:],
             )
             st[("ssum", b)] = ssum
@@ -164,7 +165,11 @@ def tile_fusionfeature_layer_t_kernel(tc, query_feature, support_feature, out_0,
             s_sb = st[("s", b)]
             for h in range(2):
                 a = adjp.tile([P, 512], F32, name="adj_ps", tag="adj")
-                nc.tensor.matmul(a[:], lhsT=qT[:, t, :], rhs=s_sb[:, h * 512:(h + 1) * 512], start=True, stop=True)
+                nc.tensor.matmul(
+                    a[:].rearrange("n (u p e) -> n u p e", u=2, e=2), lhsT=qT[:, t, :],
+                    rhs=s_sb[:, h * 512:(h + 1) * 512].rearrange("c (p u e) -> c u p e", u=2, e=2),
+                    start=True, stop=True,
+                )
                 st[("adj", i, h)] = a
 
         def max_half(i, h):
@@ -192,22 +197,21 @@ def tile_fusionfeature_layer_t_kernel(tc, query_feature, support_feature, out_0,
 
         def trans(i):
             e_sb = st[("e", i)]
-            xt = auxp.tile([P, T, P], BF16, name="xt", tag="aux")
-            for j in range(8):
-                nc.tensor.transpose(xt[:, j, :], e_sb[:, j * P:(j + 1) * P], ident[:])
+            words = e_sb[:].bitcast(F32)
+            xt = auxp.tile([P, 4, P], F32, name="xt", tag="aux")
+            for j in range(4):
+                nc.tensor.transpose(xt[:, j, :], words[:, j * P:(j + 1) * P], ident32[:])
             st[("xt", i)] = xt
 
         def cpout(i):
             t = i % T
             grp = work.tile([P, 2, P, 4], BF16, name="grp", tag="grp", align_bytes=64)
-            src = st[("xt", i)][:].rearrange("p (g j) n -> p g n j", g=2)
-            if i == NT - 1 or (t in SPLIT_CP and i < NT - 3):
-                nc.scalar.copy(out=grp[:, 0], in_=src[:, 0])
-                nc.vector.tensor_copy(out=grp[:, 1], in_=src[:, 1])
-            elif t in DVE_CP or i >= NT - 3:
-                nc.vector.tensor_copy(out=grp[:], in_=src)
+            src = st[("xt", i)][:].rearrange("p (g u) n -> p g n u", g=2)
+            dst = grp[:].bitcast(F32)
+            if t in DVE_CP:
+                nc.vector.tensor_copy(out=dst, in_=src)
             else:
-                nc.scalar.copy(out=grp[:], in_=src)
+                nc.scalar.copy(out=dst, in_=src)
             st[("grp", i)] = grp
 
         def quant(i):

@@ -41,8 +41,8 @@ def tile_fusionfeature_layer_t_kernel(tc, query_feature, support_feature, out_0,
         work = ctx.enter_context(tc.tile_pool(name="work", bufs=3))
         nap = ctx.enter_context(tc.tile_pool(name="nap", bufs=LEAD + 3))
         outp = ctx.enter_context(tc.tile_pool(name="outp", bufs=2))
-        adjp = ctx.enter_context(tc.psum_pool(name="adjp", bufs=3))
-        auxp = ctx.enter_context(tc.psum_pool(name="auxp", bufs=3))
+        adjp = ctx.enter_context(tc.psum_pool(name="adjp", bufs=4))
+        auxp = ctx.enter_context(tc.psum_pool(name="auxp", bufs=2))
         lgp = ctx.enter_context(tc.psum_pool(name="lgp", bufs=2))
         if PIN:
             ctx.enter_context(tc.manual_schedule())
@@ -74,7 +74,7 @@ def tile_fusionfeature_layer_t_kernel(tc, query_feature, support_feature, out_0,
             if lo == 0:
                 st[("qT", b)] = prep.tile([P, T, P], BF16, name="qT", tag="qT")
             qT = st[("qT", b)]
-            qT_ps = auxp.tile([P, T, P], BF16, name="qT_ps", tag="aux")
+            qT_ps = adjp.tile([P, T, P], BF16, name="qT_ps", tag="adj")
             for t in range(lo, hi):
                 nc.tensor.transpose(qT_ps[:, t, :], q_sb[:, t, :], ident[:])
             nc.scalar.copy(out=qT[:, lo:hi, :], in_=qT_ps[:, lo:hi, :])
@@ -121,7 +121,7 @@ def tile_fusionfeature_layer_t_kernel(tc, query_feature, support_feature, out_0,
         def prep_d1(b):
             qT = st[("qT", b)]
             ss3 = st[("ss3", b)]
-            v_ps = auxp.tile([P, T, 4], F32, name="v_ps", tag="aux")
+            v_ps = adjp.tile([P, T, 4], F32, name="v_ps", tag="adj")
             for t in range(T):
                 nc.tensor.matmul(v_ps[:, t, 0:3], lhsT=qT[:, t, :], rhs=ss3[:, 0:3], start=True, stop=True)
             st[("v_ps", b)] = v_ps
@@ -159,28 +159,27 @@ def tile_fusionfeature_layer_t_kernel(tc, query_feature, support_feature, out_0,
             if h == 1:
                 nc.sync.dma_start(out=o1_dram[b], in_=o1[:].rearrange("p t c -> p (t c)"))
 
-        def adj(i):
+        def adj(i, h):
             b, t = divmod(i, T)
             qT = st[("qT", b)]
             s_sb = st[("s", b)]
-            for h in range(2):
-                a = adjp.tile([P, 512], F32, name="adj_ps", tag="adj")
-                nc.tensor.matmul(
-                    a[:].rearrange("n (u p e) -> n u p e", u=2, e=2), lhsT=qT[:, t, :],
-                    rhs=s_sb[:, h * 512:(h + 1) * 512].rearrange("c (p u e) -> c u p e", u=2, e=2),
-                    start=True, stop=True,
-                )
-                st[("adj", i, h)] = a
+            a = adjp.tile([P, 512], F32, name="adj_ps", tag="adj")
+            nc.tensor.matmul(
+                a[:].rearrange("n (u p e) -> n u p e", u=2, e=2), lhsT=qT[:, t, :],
+                rhs=s_sb[:, h * 512:(h + 1) * 512].rearrange("c (p u e) -> c u p e", u=2, e=2),
+                start=True, stop=True,
+            )
+            st[("adj", i, h)] = a
 
         def max_half(i, h):
-            if h == 0:
+            if h == 1:
                 st[("na", i)] = nap.tile([P, N], F32, name="na", tag="na")
                 st[("nm", i)] = small.tile([P, 2], F32, name="nm", tag="nm", bufs=LEAD + 3)
             na = st[("na", i)]
             nm = st[("nm", i)]
             nc.vector.tensor_scalar(
                 out=na[:, h * 512:(h + 1) * 512], in0=st[("adj", i, h)][:], scalar1=-1.0,
-                scalar2=(None if h == 0 else nm[:, 0:1]), op0=ALU.mult, op1=ALU.min,
+                scalar2=(None if h == 1 else nm[:, 1:2]), op0=ALU.mult, op1=ALU.min,
                 accum_out=nm[:, h:h + 1],
             )
 
@@ -190,7 +189,7 @@ def tile_fusionfeature_layer_t_kernel(tc, query_feature, support_feature, out_0,
                 st[("rs", b)] = small.tile([P, T], F32, name="rs", tag="rs")
             e_sb = work.tile([P, N], BF16, name="e_sb", tag="e")
             nc.scalar.activation(
-                out=e_sb[:], in_=st[("na", i)][:], func=ACTF.Exp, bias=st[("nm", i)][:, 1:2], scale=-1.0,
+                out=e_sb[:], in_=st[("na", i)][:], func=ACTF.Exp, bias=st[("nm", i)][:, 0:1], scale=-1.0,
                 accum_out=st[("rs", b)][:, t:t + 1],
             )
             st[("e", i)] = e_sb
@@ -299,16 +298,18 @@ def tile_fusionfeature_layer_t_kernel(tc, query_feature, support_feature, out_0,
                 pb, pu = divmod(s - 2, T)
                 if pb + 1 < B:
                     preps.append((pb + 1, pu))
-            if 0 <= s - 1 < NT:
-                trans(s - 1)
             if 0 <= s + LEAD + 1 < NT:
-                adj(s + LEAD + 1)
-            if s == first:
-                prep_a(0, 1, T)
+                adj(s + LEAD + 1, 0)
             if 0 <= s - 4 < NT:
                 mxmm(s - 4)
+            if 0 <= s + LEAD + 1 < NT:
+                adj(s + LEAD + 1, 1)
+            if s == first:
+                prep_a(0, 1, T)
+            if 0 <= s - 1 < NT:
+                trans(s - 1)
             if 0 <= s + LEAD < NT:
-                max_half(s + LEAD, 0)
+                max_half(s + LEAD, 1)
             for pb, pu in preps:
                 prep_step_dve(pb, pu)
             gl = s - 3
@@ -317,7 +318,7 @@ def tile_fusionfeature_layer_t_kernel(tc, query_feature, support_feature, out_0,
             if 0 <= s - 3 < NT:
                 quant(s - 3)
             if 0 <= s + LEAD < NT:
-                max_half(s + LEAD, 1)
+                max_half(s + LEAD, 0)
             if 0 <= s < NT:
                 expo(s)
             if 0 <= s - 2 < NT:

@@ -74,7 +74,7 @@ def tile_fusionfeature_layer_t_kernel(tc, query_feature, support_feature, out_0,
             if lo == 0:
                 st[("qT", b)] = prep.tile([P, T, P], BF16, name="qT", tag="qT")
             qT = st[("qT", b)]
-            qT_ps = adjp.tile([P, T, P], BF16, name="qT_ps", tag="adj")
+            qT_ps = auxp.tile([P, T, P], BF16, name="qT_ps", tag="aux")
             for t in range(lo, hi):
                 nc.tensor.transpose(qT_ps[:, t, :], q_sb[:, t, :], ident[:])
             nc.scalar.copy(out=qT[:, lo:hi, :], in_=qT_ps[:, lo:hi, :])
@@ -121,7 +121,7 @@ def tile_fusionfeature_layer_t_kernel(tc, query_feature, support_feature, out_0,
         def prep_d1(b):
             qT = st[("qT", b)]
             ss3 = st[("ss3", b)]
-            v_ps = adjp.tile([P, T, 4], F32, name="v_ps", tag="adj")
+            v_ps = auxp.tile([P, T, 4], F32, name="v_ps", tag="aux")
             for t in range(T):
                 nc.tensor.matmul(v_ps[:, t, 0:3], lhsT=qT[:, t, :], rhs=ss3[:, 0:3], start=True, stop=True)
             st[("v_ps", b)] = v_ps

@@ -22,7 +22,6 @@ FLOPS = 2 * 2 * B * N * N * C
 
 PIN = True
 LEAD = 2
-DVE_CP = ()
 
 
 def tile_fusionfeature_layer_t_kernel(tc, query_feature, support_feature, out_0, out_1):
@@ -62,8 +61,11 @@ def tile_fusionfeature_layer_t_kernel(tc, query_feature, support_feature, out_0,
             q_sb = inp.tile([P, T, C], BF16, name="q_sb", tag="q")
             s_sb = inp.tile([P, N], BF16, name="s_sb", tag="s")
             q2 = inp.tile([P, 2, 4, C], BF16, name="q2", tag="q2")
-            nc.sync.dma_start(out=q_sb[:].rearrange("p t c -> p (t c)"), in_=q_dram[b])
+            head = 1 if b == 0 else T
+            nc.sync.dma_start(out=q_sb[:, 0:head].rearrange("p t c -> p (t c)"), in_=q_dram[b][:, 0:head * C])
             nc.sync.dma_start(out=s_sb[:], in_=s_dram[b])
+            if head < T:
+                nc.sync.dma_start(out=q_sb[:, head:T].rearrange("p t c -> p (t c)"), in_=q_dram[b][:, head * C:])
             nc.sync.dma_start(out=q2[:].rearrange("p g j c -> p g (j c)"), in_=q2_dram[b])
             st[("q", b)] = q_sb
             st[("s", b)] = s_sb
@@ -73,11 +75,13 @@ def tile_fusionfeature_layer_t_kernel(tc, query_feature, support_feature, out_0,
             q_sb = st[("q", b)]
             if lo == 0:
                 st[("qT", b)] = prep.tile([P, T, P], BF16, name="qT", tag="qT")
-            qT = st[("qT", b)]
             qT_ps = auxp.tile([P, T, P], BF16, name="qT_ps", tag="aux")
             for t in range(lo, hi):
                 nc.tensor.transpose(qT_ps[:, t, :], q_sb[:, t, :], ident[:])
-            nc.scalar.copy(out=qT[:, lo:hi, :], in_=qT_ps[:, lo:hi, :])
+            st[("qT_ps", b)] = qT_ps
+
+        def prep_a_copy(b, lo, hi):
+            nc.scalar.copy(out=st[("qT", b)][:, lo:hi, :], in_=st[("qT_ps", b)][:, lo:hi, :])
 
         def prep_regroup(b):
             q2 = st[("q2", b)]
@@ -134,8 +138,11 @@ def tile_fusionfeature_layer_t_kernel(tc, query_feature, support_feature, out_0,
         def prep_d2_act(b):
             en = small.tile([P, T], F32, name="en", tag="en")
             nc.scalar.activation(out=en[:], in_=st[("v", b)][:], func=ACTF.Exp, scale=-1.0)
+            st[("en", b)] = en
+
+        def prep_den(b):
             d = small.tile([P, T], F32, name="d", tag="d")
-            nc.gpsimd.tensor_scalar(out=d[:], in0=en[:], scalar1=1.0, scalar2=1.0, op0=ALU.mult, op1=ALU.add)
+            nc.gpsimd.tensor_scalar(out=d[:], in0=st[("en", b)][:], scalar1=1.0, scalar2=1.0, op0=ALU.mult, op1=ALU.add)
             st[("d", b)] = d
 
         def prep_d3(b):
@@ -203,11 +210,10 @@ def tile_fusionfeature_layer_t_kernel(tc, query_feature, support_feature, out_0,
             st[("xt", i)] = xt
 
         def cpout(i):
-            t = i % T
             grp = work.tile([P, 2, P, 4], BF16, name="grp", tag="grp", align_bytes=64)
             src = st[("xt", i)][:].rearrange("p (g u) n -> p g n u", g=2)
             dst = grp[:].bitcast(F32)
-            if t in DVE_CP:
+            if NT - 3 <= i < NT - 1:
                 nc.vector.tensor_copy(out=dst, in_=src)
             else:
                 nc.scalar.copy(out=dst, in_=src)
@@ -249,17 +255,21 @@ def tile_fusionfeature_layer_t_kernel(tc, query_feature, support_feature, out_0,
             nc.vector.reciprocal(out=gg[:], in_=st[("dr", b, h)][:])
             st[("gg", b, h)] = gg
 
-        def fin(b, h):
+        def fin(b, h, lo, hi):
             gg = st[("gg", b, h)]
             lg = st[("lg", b, h)]
             q_sb = st[("q", b)]
-            o0 = outp.tile([P, 4, C], F32, name="o0", tag="o0", bufs=3)
-            for k in range(4):
+            if lo == 0:
+                st[("o0", b, h)] = outp.tile([P, 4, C], F32, name="o0", tag="o0", bufs=3)
+            o0 = st[("o0", b, h)]
+            for k in range(lo, hi):
                 nc.vector.scalar_tensor_tensor(
                     out=o0[:, k, :], in0=lg[:, k, :], scalar=gg[:, k:k + 1], in1=q_sb[:, 4 * h + k, :],
                     op0=ALU.mult, op1=ALU.add,
                 )
-            nc.sync.dma_start(out=o0_dram[b][:, h * 512:(h + 1) * 512], in_=o0[:].rearrange("p k c -> p (k c)"))
+            nc.sync.dma_start(
+                out=o0_dram[b][:, h * 512 + lo * C:h * 512 + hi * C], in_=o0[:, lo:hi].rearrange("p k c -> p (k c)")
+            )
 
         def prep_step(b, u):
             if u == 0 and b > 0:
@@ -271,9 +281,8 @@ def tile_fusionfeature_layer_t_kernel(tc, query_feature, support_feature, out_0,
             if u == 2:
                 prep_regroup(b)
                 prep_d1(b)
-            if u == 3:
-                prep_d2_act(b)
             if u == 4:
+                prep_den(b)
                 prep_quant(b)
             if u == 6:
                 out1(b, 0)
@@ -283,13 +292,14 @@ def tile_fusionfeature_layer_t_kernel(tc, query_feature, support_feature, out_0,
         def prep_step_dve(b, u):
             if u == 3:
                 prep_d2_dve(b)
-            if u == 5:
+            if u == 6:
                 prep_d3(b)
 
         first = -LEAD - 1
         load(0)
         load(1)
         prep_a(0, 0, 1)
+        prep_a_copy(0, 0, 1)
         for s in range(first, NT + 7):
             preps = []
             if 0 <= s - first - 1 < T:
@@ -306,6 +316,7 @@ def tile_fusionfeature_layer_t_kernel(tc, query_feature, support_feature, out_0,
                 adj(s + LEAD + 1, 1)
             if s == first:
                 prep_a(0, 1, T)
+                prep_a_copy(0, 1, T)
             if 0 <= s - 1 < NT:
                 trans(s - 1)
             if 0 <= s + LEAD < NT:
@@ -321,14 +332,23 @@ def tile_fusionfeature_layer_t_kernel(tc, query_feature, support_feature, out_0,
                 max_half(s + LEAD, 0)
             if 0 <= s < NT:
                 expo(s)
+            for pb, pu in preps:
+                if pu == 2 and pb > 0:
+                    prep_a_copy(pb, 0, T)
+                if pu == 4:
+                    prep_d2_act(pb)
             if 0 <= s - 2 < NT:
                 cpout(s - 2)
             dl = s - 1
             if 0 <= dl < NT and dl % 4 == 3:
                 fin_dr(dl // T, (dl % T) // 4)
             fl = s - 5
-            if 0 <= fl < NT and fl % 4 == 3:
-                fin(fl // T, (fl % T) // 4)
+            if 0 <= fl < NT - 1 and fl % 4 == 3:
+                fin(fl // T, (fl % T) // 4, 0, 4)
+            if fl == NT - 2:
+                fin(B - 1, 1, 0, 3)
+            if fl == NT - 1:
+                fin(B - 1, 1, 3, 4)
             if 0 <= s and s % T == 0 and s // T + 2 < B:
                 load(s // T + 2)
             for pb, pu in preps:

from contextlib import ExitStack

import concourse.mybir as mybir
from concourse.masks import make_identity

F32 = mybir.dt.float32
BF16 = mybir.dt.bfloat16
U32 = mybir.dt.uint32
U8 = mybir.dt.uint8
FP8X4 = mybir.dt.float8_e4m3fn_x4
ACTF = mybir.ActivationFunctionType
ALU = mybir.AluOpType
AX = mybir.AxisListType

B = 16
P = 128
N = 1024
C = 128
T = N // P
NT = B * T
FLOPS = 2 * 2 * B * N * N * C

PIN = True
LEAD = 2


def tile_fusionfeature_layer_t_kernel(tc, query_feature, support_feature, out_0, out_1):
    nc = tc.nc
    q_dram = query_feature.rearrange("b c h w -> b c (h w)")
    s_dram = support_feature.rearrange("b c h w -> b c (h w)")
    q2_dram = query_feature.rearrange("b (g ch) (cl tx) w -> b (ch cl) g (tx w)", g=2, cl=2)
    o0_dram = out_0.rearrange("b c h w -> b c (h w)")
    o1_dram = out_1.rearrange("b c h w -> b c (h w)")

    with ExitStack() as ctx:
        const = ctx.enter_context(tc.tile_pool(name="const", bufs=1))
        inp = ctx.enter_context(tc.tile_pool(name="inp", bufs=4))
        prep = ctx.enter_context(tc.tile_pool(name="prep", bufs=2))
        small = ctx.enter_context(tc.tile_pool(name="small", bufs=3))
        work = ctx.enter_context(tc.tile_pool(name="work", bufs=3))
        nap = ctx.enter_context(tc.tile_pool(name="nap", bufs=LEAD + 3))
        outp = ctx.enter_context(tc.tile_pool(name="outp", bufs=2))
        adjp = ctx.enter_context(tc.psum_pool(name="adjp", bufs=4))
        auxp = ctx.enter_context(tc.psum_pool(name="auxp", bufs=2))
        lgp = ctx.enter_context(tc.psum_pool(name="lgp", bufs=2))
        if PIN:
            ctx.enter_context(tc.manual_schedule())

        ident = const.tile([P, P], BF16, name="ident")
        make_identity(nc, ident[:])
        ident32 = const.tile([P, P], F32, name="ident32")
        make_identity(nc, ident32[:])
        junk = const.tile([P, 512], F32, name="junk")
        warm = const.tile([P, 2], F32, name="warm")
        nc.vector.memset(warm[:, 0:1], 0.0)
        nc.scalar.activation(out=warm[:, 1:2], in_=warm[:, 0:1], func=ACTF.Exp)

        st = {}

        def load(b):
            q_sb = inp.tile([P, T, C], BF16, name="q_sb", tag="q")
            s_sb = inp.tile([P, N], BF16, name="s_sb", tag="s")
            q2 = inp.tile([P, 2, 4, C], BF16, name="q2", tag="q2")
            head = 1 if b == 0 else T
            nc.sync.dma_start(out=q_sb[:, 0:head].rearrange("p t c -> p (t c)"), in_=q_dram[b][:, 0:head * C])
            nc.sync.dma_start(out=s_sb[:], in_=s_dram[b])
            if head < T:
                nc.sync.dma_start(out=q_sb[:, head:T].rearrange("p t c -> p (t c)"), in_=q_dram[b][:, head * C:])
            nc.sync.dma_start(out=q2[:].rearrange("p g j c -> p g (j c)"), in_=q2_dram[b])
            st[("q", b)] = q_sb
            st[("s", b)] = s_sb
            st[("q2", b)] = q2

        def prep_a(b, lo, hi):
            q_sb = st[("q", b)]
            if lo == 0:
                st[("qT", b)] = prep.tile([P, T, P], BF16, name="qT", tag="qT")
            qT_ps = auxp.tile([P, T, P], BF16, name="qT_ps", tag="aux")
            for t in range(lo, hi):
                nc.tensor.transpose(qT_ps[:, t, :], q_sb[:, t, :], ident[:])
            st[("qT_ps", b)] = qT_ps

        def prep_a_copy(b, lo, hi):
            nc.scalar.copy(out=st[("qT", b)][:, lo:hi, :], in_=st[("qT_ps", b)][:, lo:hi, :])

        def prep_regroup(b):
            q2 = st[("q2", b)]
            qg = prep.tile([P, 2, C, 4], BF16, name="qg", tag="qg", align_bytes=64)
            for g in range(2):
                nc.gpsimd.tensor_scalar(
                    out=qg[:, g], in0=q2[:, g].rearrange("p j c -> p c j"),
                    scalar1=1.0, scalar2=0.0, op0=ALU.mult, op1=ALU.add,
                )
            st[("qg", b)] = qg

        def prep_ssum(b):
            ssum = small.tile([P, 1], F32, name="ssum", tag="ssum")
            nc.vector.scalar_tensor_tensor(
                out=junk[:], in0=st[("s", b)][:, 0:512], scalar=1.0, in1=st[("s", b)][:, 512:1024],
                op0=ALU.mult, op1=ALU.add, accum_out=ssum[:],
            )
            st[("ssum", b)] = ssum

        def prep_quant(b):
            qg = st[("qg", b)]
            qc = prep.tile([P, 2 * C], U32, name="qc", tag="qc", align_bytes=64)
            qs = prep.tile([P, 2 * C], U8, name="qs", tag="qs", align_bytes=64)
            nc.vector.quantize_mx(
                out=qc[:].bitcast(FP8X4), scales=qs[:], in_=qg[:].rearrange("p g c j -> p (g c j)")
            )
            st[("qc", b)] = qc
            st[("qs", b)] = qs

        def prep_split(b):
            ssum = st[("ssum", b)]
            ss3 = small.tile([P, 4], BF16, name="ss3", tag="ss3")
            rr = small.tile([P, 2], F32, name="rr", tag="rr")
            nc.gpsimd.tensor_copy(out=ss3[:, 0:1], in_=ssum[:])
            nc.gpsimd.tensor_tensor(out=rr[:, 0:1], in0=ssum[:], in1=ss3[:, 0:1], op=ALU.subtract)
            nc.gpsimd.tensor_copy(out=ss3[:, 1:2], in_=rr[:, 0:1])
            nc.gpsimd.tensor_tensor(out=rr[:, 1:2], in0=rr[:, 0:1], in1=ss3[:, 1:2], op=ALU.subtract)
            nc.gpsimd.tensor_copy(out=ss3[:, 2:3], in_=rr[:, 1:2])
            st[("ss3", b)] = ss3

        def prep_d1(b):
            qT = st[("qT", b)]
            ss3 = st[("ss3", b)]
            v_ps = auxp.tile([P, T, 4], F32, name="v_ps", tag="aux")
            for t in range(T):
                nc.tensor.matmul(v_ps[:, t, 0:3], lhsT=qT[:, t, :], rhs=ss3[:, 0:3], start=True, stop=True)
            st[("v_ps", b)] = v_ps

        def prep_d2_dve(b):
            v = small.tile([P, T], F32, name="v", tag="v")
            nc.vector.tensor_reduce(out=v[:], in_=st[("v_ps", b)][:, :, 0:3], axis=AX.X, op=ALU.add)
            st[("v", b)] = v

        def prep_d2_act(b):
            en = small.tile([P, T], F32, name="en", tag="en")
            nc.scalar.activation(out=en[:], in_=st[("v", b)][:], func=ACTF.Exp, scale=-1.0)
            st[("en", b)] = en

        def prep_den(b):
            d = small.tile([P, T], F32, name="d", tag="d")
            nc.gpsimd.tensor_scalar(out=d[:], in0=st[("en", b)][:], scalar1=1.0, scalar2=1.0, op0=ALU.mult, op1=ALU.add)
            st[("d", b)] = d

        def prep_d3(b):
            gate = small.tile([P, T], F32, name="gate", tag="gate")
            nc.vector.reciprocal(out=gate[:], in_=st[("d", b)][:])
            gate1 = small.tile([P, T], F32, name="gate1", tag="gate1")
            nc.gpsimd.tensor_scalar(out=gate1[:], in0=gate[:], scalar1=1.0, scalar2=1.0, op0=ALU.mult, op1=ALU.add)
            st[("gate1", b)] = gate1

        def out1(b, h):
            s_sb = st[("s", b)]
            gate1 = st[("gate1", b)]
            if h == 0:
                st[("o1", b)] = outp.tile([P, T, C], F32, name="o1", tag="o1")
            o1 = st[("o1", b)]
            for t in range(4 * h, 4 * h + 4):
                nc.gpsimd.tensor_scalar(
                    out=o1[:, t, :], in0=s_sb[:, t * C:(t + 1) * C],
                    scalar1=gate1[:, t:t + 1], scalar2=0.0, op0=ALU.mult, op1=ALU.add,
                )
            if h == 1:
                nc.sync.dma_start(out=o1_dram[b], in_=o1[:].rearrange("p t c -> p (t c)"))

        def adj(i, h):
            b, t = divmod(i, T)
            qT = st[("qT", b)]
            s_sb = st[("s", b)]
            a = adjp.tile([P, 512], F32, name="adj_ps", tag="adj")
            nc.tensor.matmul(
                a[:].rearrange("n (u p e) -> n u p e", u=2, e=2), lhsT=qT[:, t, :],
                rhs=s_sb[:, h * 512:(h + 1) * 512].rearrange("c (p u e) -> c u p e", u=2, e=2),
                start=True, stop=True,
            )
            st[("adj", i, h)] = a

        def max_half(i, h):
            if h == 1:
                st[("na", i)] = nap.tile([P, N], F32, name="na", tag="na")
                st[("nm", i)] = small.tile([P, 2], F32, name="nm", tag="nm", bufs=LEAD + 3)
            na = st[("na", i)]
            nm = st[("nm", i)]
            nc.vector.tensor_scalar(
                out=na[:, h * 512:(h + 1) * 512], in0=st[("adj", i, h)][:], scalar1=-1.0,
                scalar2=(None if h == 1 else nm[:, 1:2]), op0=ALU.mult, op1=ALU.min,
                accum_out=nm[:, h:h + 1],
            )

        def expo(i):
            b, t = divmod(i, T)
            if t == 0:
                st[("rs", b)] = small.tile([P, T], F32, name="rs", tag="rs")
            e_sb = work.tile([P, N], BF16, name="e_sb", tag="e")
            nc.scalar.activation(
                out=e_sb[:], in_=st[("na", i)][:], func=ACTF.Exp, bias=st[("nm", i)][:, 0:1], scale=-1.0,
                accum_out=st[("rs", b)][:, t:t + 1],
            )
            st[("e", i)] = e_sb

        def trans(i):
            e_sb = st[("e", i)]
            words = e_sb[:].bitcast(F32)
            xt = auxp.tile([P, 4, P], F32, name="xt", tag="aux")
            for j in range(4):
                nc.tensor.transpose(xt[:, j, :], words[:, j * P:(j + 1) * P], ident32[:])
            st[("xt", i)] = xt

        def cpout(i):
            grp = work.tile([P, 2, P, 4], BF16, name="grp", tag="grp", align_bytes=64)
            src = st[("xt", i)][:].rearrange("p (g u) n -> p g n u", g=2)
            dst = grp[:].bitcast(F32)
            if NT - 3 <= i < NT - 1:
                nc.vector.tensor_copy(out=dst, in_=src)
            else:
                nc.scalar.copy(out=dst, in_=src)
            st[("grp", i)] = grp

        def quant(i):
            ec = work.tile([P, 2 * P], U32, name="ec", tag="ec", align_bytes=64)
            es = work.tile([P, 2 * P], U8, name="es", tag="es", align_bytes=64)
            nc.vector.quantize_mx(
                out=ec[:].bitcast(FP8X4), scales=es[:], in_=st[("grp", i)][:].rearrange("p g n j -> p (g n j)")
            )
            st[("ec", i)] = ec
            st[("es", i)] = es

        def mxmm(i):
            b, t = divmod(i, T)
            if t % 4 == 0:
                st[("lg", b, t // 4)] = lgp.tile([P, 4, C], F32, name="lg", tag="lg")
            lg = st[("lg", b, t // 4)]
            ec = st[("ec", i)]
            es = st[("es", i)]
            qc = st[("qc", b)]
            qs = st[("qs", b)]
            for g in range(2):
                sl = slice(g * P, (g + 1) * P)
                nc.tensor.matmul_mx(
                    out=lg[:, t % 4, :], lhsT=ec[:, sl].bitcast(FP8X4), lhsT_scale=es[:, sl],
                    rhs=qc[:, sl].bitcast(FP8X4), rhs_scale=qs[:, sl], start=(g == 0), stop=(g == 1),
                )

        def fin_dr(b, h):
            sl = slice(4 * h, 4 * h + 4)
            dr = small.tile([P, 4], F32, name="dr", tag="dr")
            nc.gpsimd.tensor_tensor(out=dr[:], in0=st[("d", b)][:, sl], in1=st[("rs", b)][:, sl], op=ALU.mult)
            st[("dr", b, h)] = dr

        def fin_gg(b, h):
            gg = small.tile([P, 4], F32, name="gg", tag="gg")
            nc.vector.reciprocal(out=gg[:], in_=st[("dr", b, h)][:])
            st[("gg", b, h)] = gg

        def fin(b, h, lo, hi):
            gg = st[("gg", b, h)]
            lg = st[("lg", b, h)]
            q_sb = st[("q", b)]
            if lo == 0:
                st[("o0", b, h)] = outp.tile([P, 4, C], F32, name="o0", tag="o0", bufs=3)
            o0 = st[("o0", b, h)]
            for k in range(lo, hi):
                nc.vector.scalar_tensor_tensor(
                    out=o0[:, k, :], in0=lg[:, k, :], scalar=gg[:, k:k + 1], in1=q_sb[:, 4 * h + k, :],
                    op0=ALU.mult, op1=ALU.add,
                )
            nc.sync.dma_start(
                out=o0_dram[b][:, h * 512 + lo * C:h * 512 + hi * C], in_=o0[:, lo:hi].rearrange("p k c -> p (k c)")
            )

        def prep_step(b, u):
            if u == 0 and b > 0:
                prep_a(b, 0, T)
            if u == 0:
                prep_ssum(b)
            if u == 1:
                prep_split(b)
            if u == 2:
                prep_regroup(b)
                prep_d1(b)
            if u == 4:
                prep_den(b)
                prep_quant(b)
            if u == 6:
                out1(b, 0)
            if u == 7:
                out1(b, 1)

        def prep_step_dve(b, u):
            if u == 3:
                prep_d2_dve(b)
            if u == 6:
                prep_d3(b)

        first = -LEAD - 1
        load(0)
        load(1)
        prep_a(0, 0, 1)
        prep_a_copy(0, 0, 1)
        for s in range(first, NT + 7):
            preps = []
            if 0 <= s - first - 1 < T:
                preps.append((0, s - first - 1))
            if s >= 2:
                pb, pu = divmod(s - 2, T)
                if pb + 1 < B:
                    preps.append((pb + 1, pu))
            if 0 <= s + LEAD + 1 < NT:
                adj(s + LEAD + 1, 0)
            if 0 <= s - 4 < NT:
                mxmm(s - 4)
            if 0 <= s + LEAD + 1 < NT:
                adj(s + LEAD + 1, 1)
            if s == first:
                prep_a(0, 1, T)
                prep_a_copy(0, 1, T)
            if 0 <= s - 1 < NT:
                trans(s - 1)
            if 0 <= s + LEAD < NT:
                max_half(s + LEAD, 1)
            for pb, pu in preps:
                prep_step_dve(pb, pu)
            gl = s - 3
            if 0 <= gl < NT and gl % 4 == 3:
                fin_gg(gl // T, (gl % T) // 4)
            if 0 <= s - 3 < NT:
                quant(s - 3)
            if 0 <= s + LEAD < NT:
                max_half(s + LEAD, 0)
            if 0 <= s < NT:
                expo(s)
            for pb, pu in preps:
                if pu == 2 and pb > 0:
                    prep_a_copy(pb, 0, T)
                if pu == 4:
                    prep_d2_act(pb)
            if 0 <= s - 2 < NT:
                cpout(s - 2)
            dl = s - 1
            if 0 <= dl < NT and dl % 4 == 3:
                fin_dr(dl // T, (dl % T) // 4)
            fl = s - 5
            if 0 <= fl < NT - 1 and fl % 4 == 3:
                fin(fl // T, (fl % T) // 4, 0, 4)
            if fl == NT - 2:
                fin(B - 1, 1, 0, 3)
            if fl == NT - 1:
                fin(B - 1, 1, 3, 4)
            if 0 <= s and s % T == 0 and s // T + 2 < B:
                load(s // T + 2)
            for pb, pu in preps:
                prep_step(pb, pu)
